import numpy as np
import ml_dtypes


def mxq(x, axis, fmt="e4m3"):
    dtype, down = {"e4m3": (ml_dtypes.float8_e4m3fn, 7), "e5m2": (ml_dtypes.float8_e5m2, 14)}[fmt]
    v = np.moveaxis(np.asarray(x, np.float32).astype(ml_dtypes.bfloat16).astype(np.float64), axis, -1)
    blocks = v.reshape(v.shape[:-1] + (-1, 32))
    amax = np.abs(blocks).max(-1, keepdims=True)
    byte = np.maximum(np.where(amax > 0, np.frexp(amax)[1] - 1 + 127, 0) - down, 1)
    scale = np.exp2(byte - 127.0)
    codes = (blocks / scale).astype(np.float32).astype(dtype).astype(np.float64)
    return np.moveaxis((codes * scale).reshape(v.shape), -1, axis)


WIDE = False


def mx_kscale(k):
    if not WIDE:
        return np.ones(k)
    levels = np.array([10, -10, 5, -5, 0])
    a = np.random.permutation(np.resize(levels, k // 512 * 4)).reshape(k // 512, 4)
    idx = np.arange(k)
    return np.exp2(a[idx // 512, idx % 128 // 32])


BF16 = ml_dtypes.bfloat16


def bf(x):
    return np.asarray(x, np.float32).astype(BF16)


def f64(x):
    return np.asarray(x).astype(np.float64)


B, N, L, H, S, R, C = 4, 1024, 4, 64, 2, 2, 512
M = R * S * H
BN_EPS = 1e-5


def setup_inputs():
    s = mx_kscale(L * M).reshape(L, M)
    t = mx_kscale(C)
    return {"hops": bf((1.7 * np.random.standard_normal((B, N, L, M)) + 0.4 * np.random.standard_normal((L, M))) * s),
            "weight": bf(np.random.standard_normal((L, M, C)) * 0.6 / np.sqrt(L * M) / s[:, :, None]),
            "gamma": bf((1.0 + 0.1 * np.random.standard_normal(C)) * t),
            "beta": bf(0.2 * np.random.standard_normal(C) * t),
            "w2": bf(np.random.standard_normal((C, C)) / np.sqrt(C) / t[None, :]),
            "b2": bf(0.2 * np.random.standard_normal(C))}


def reference(hops, weight, gamma, beta, w2, b2):
    hf = f64(hops).reshape(B * N, L * M)
    wm = f64(weight).reshape(L * M, C)
    flat = mxq(hf, 1, "e4m3") @ mxq(wm, 0, "e4m3")
    mean = flat.mean(axis=0)
    var = flat.var(axis=0)
    normed = (flat - mean) * (1.0 / np.sqrt(var + BN_EPS)) * f64(gamma) + f64(beta)
    y = np.maximum(normed, 0.0)
    out = (mxq(y, 1, "e4m3") @ mxq(f64(w2), 1, "e4m3").T) + f64(b2)
    return out.reshape(B, N, C)

@@ -1,0 +1,264 @@
+from contextlib import ExitStack
+
+import concourse.mybir as mybir
+from concourse.masks import make_identity
+
+F32 = mybir.dt.float32
+BF16 = mybir.dt.bfloat16
+U32 = mybir.dt.uint32
+U8 = mybir.dt.uint8
+FP8X4 = mybir.dt.float8_e4m3fn_x4
+ACT = mybir.ActivationFunctionType
+ALU = mybir.AluOpType
+
+P = 128
+ROWS = 4096
+K1 = 1024
+C = 512
+GROUP = 512
+NG = ROWS // GROUP
+IN_PSUM = (6, 7)
+BN_EPS = 1e-5
+FLOPS = 2 * ROWS * K1 * C + 2 * ROWS * C * C
+MANUAL = True
+
+
+def tile_ginconvfft_pb_t_kernel(tc, hops, weight, gamma, beta, w2, b2, out):
+    nc = tc.nc
+    hflat = hops.rearrange("b n l m -> (b n) (l m)")
+    wflat = weight.rearrange("l m c -> (l m) c")
+    oflat = out.rearrange("b n o -> (b n) o")
+
+    with ExitStack() as ctx:
+        if MANUAL:
+            ctx.enter_context(tc.manual_schedule())
+        consts = ctx.enter_context(tc.tile_pool(name="consts", bufs=1))
+        raws = ctx.enter_context(tc.tile_pool(name="raws", bufs=5))
+        grps = ctx.enter_context(tc.tile_pool(name="grps", bufs=3))
+        hq = ctx.enter_context(tc.tile_pool(name="hq", bufs=3))
+        zpool = ctx.enter_context(tc.tile_pool(name="zpool", bufs=1))
+        ypool = ctx.enter_context(tc.tile_pool(name="ypool", bufs=3))
+        opool = ctx.enter_context(tc.tile_pool(name="opool", bufs=3))
+        psum = ctx.enter_context(tc.psum_pool(name="psum", bufs=4))
+
+        eps = consts.tile([P, 1], F32, name="eps")
+        nc.vector.memset(eps[:], BN_EPS)
+        junk = consts.tile([P, 1], F32, name="junk")
+        ident_f = consts.tile([P, P], F32, name="ident_f")
+        make_identity(nc, ident_f[:])
+        ident_b = consts.tile([P, P], BF16, name="ident_b")
+        make_identity(nc, ident_b[:])
+        gbraw = consts.tile([P, P], BF16, name="gbraw")
+        nc.gpsimd.memset(gbraw[:], 0.0)
+
+        wraw = raws.tile([P, 4096], BF16, name="wraw", tag="raw")
+        wview = wflat.rearrange("(a p e) c -> p a (e c)", a=4, p=P, e=2)
+        for g2 in range(2):
+            nc.sync.dma_start(
+                out=wraw[:, g2 * 2048 : (g2 + 1) * 2048].rearrange("p (a x) -> p a x", a=2),
+                in_=wview[:, 2 * g2 : 2 * g2 + 2, :],
+            )
+        hraw = []
+
+        def load_group(g):
+            t = raws.tile([P, 4096], BF16, name="hraw%d" % g, tag="raw")
+            src = hflat[g * GROUP : (g + 1) * GROUP, :].rearrange("(p t) k -> p (t k)", t=4)
+            if g == 0:
+                nc.sync.dma_start(out=t[:, 0:2048], in_=src[:, 0:2048])
+                nc.sync.dma_start(out=t[:, 2048:4096], in_=src[:, 2048:4096])
+            else:
+                nc.sync.dma_start(out=t[:], in_=src)
+            hraw.append(t)
+
+        for g in range(4):
+            load_group(g)
+
+        w2raw = consts.tile([P, 2048], BF16, name="w2raw")
+        nc.scalar.dma_start(
+            out=w2raw[:].rearrange("p (a c) -> p a c", a=4),
+            in_=w2.rearrange("(a p) c -> p a c", p=P),
+        )
+        nc.scalar.dma_start(out=gbraw[0:4, :], in_=gamma.rearrange("(t p) -> t p", p=P))
+        nc.scalar.dma_start(out=gbraw[4:8, :], in_=beta.rearrange("(t p) -> t p", p=P))
+        nc.scalar.activation(out=junk[:], in_=eps[:], func=ACT.Sqrt)
+
+        hgrp = {}
+        hcodes = {}
+        hscales = {}
+
+        def transposes(g):
+            rawf = hraw[g][:].bitcast(F32)
+            grp = grps.tile([P, 4096], BF16, name="hgrp%d" % g, tag="grp", align_bytes=64)
+            grpf = grp[:].bitcast(F32)
+            for h in range(2):
+                for g2 in range(2):
+                    xt = psum.tile([P, 512], F32, name="xt%d_%d%d" % (g, h, g2), tag="xt")
+                    for u in range(2):
+                        for tt in range(2):
+                            col = (2 * h + tt) * 512 + (2 * g2 + u) * P
+                            nc.tensor.transpose(
+                                xt[:, (2 * u + tt) * P : (2 * u + tt + 1) * P],
+                                rawf[:, col : col + P],
+                                ident_f[:],
+                            )
+                    lo = g2 * 1024 + h * 512
+                    nc.scalar.copy(
+                        out=grpf[:, lo : lo + 512].rearrange("p (x u) -> p x u", u=2),
+                        in_=xt[:].rearrange("p (u x) -> p x u", u=2),
+                    )
+            hgrp[g] = grp
+
+        def quant_hops(g):
+            codes = hq.tile([P, 1024], U32, name="hc%d" % g, tag="hc", align_bytes=64)
+            scales = hq.tile([P, 1024], U8, name="hs%d" % g, tag="hs", align_bytes=64)
+            nc.vector.quantize_mx(out=codes[:].bitcast(FP8X4), scales=scales[:], in_=hgrp[g][:])
+            hcodes[g] = codes
+            hscales[g] = scales
+
+        wc = consts.tile([P, 1024], U32, name="wc", align_bytes=64)
+        ws = consts.tile([P, 1024], U8, name="ws", align_bytes=64)
+        stats = consts.tile([P, 4 * NG * 6], F32, name="stats")
+        zsrc = {}
+
+        def matmul1(g):
+            in_psum = g in IN_PSUM
+            if not in_psum:
+                zt = zpool.tile([P, 2048], F32, name="z%d" % g)
+            for T in range(4):
+                acc = psum.tile(
+                    [P, 512], F32, name="acc%d_%d" % (g, T), tag=("xt" if g == NG - 1 else "acc")
+                )
+                for g2 in range(2):
+                    wsl = slice(g2 * 512 + T * P, g2 * 512 + (T + 1) * P)
+                    hsl = slice(g2 * 512, (g2 + 1) * 512)
+                    nc.tensor.matmul_mx(
+                        out=acc[:],
+                        lhsT=wc[:, wsl].bitcast(FP8X4),
+                        lhsT_scale=ws[:, wsl],
+                        rhs=hcodes[g][:, hsl].bitcast(FP8X4),
+                        rhs_scale=hscales[g][:, hsl],
+                        start=(g2 == 0),
+                        stop=(g2 == 1),
+                    )
+                if in_psum:
+                    zsrc[(g, T)] = acc[:]
+                else:
+                    nc.scalar.copy(out=zt[:, T * 512 : (T + 1) * 512], in_=acc[:])
+                    zsrc[(g, T)] = zt[:, T * 512 : (T + 1) * 512]
+                k = (T * NG + g) * 6
+                nc.vector.bn_stats(out=stats[:, k : k + 6], in_=zsrc[(g, T)])
+
+        wgrp = grps.tile([P, 4096], BF16, name="wgrp", tag="grp", align_bytes=64)
+        for g2 in range(2):
+            sl = slice(g2 * 2048, (g2 + 1) * 2048)
+            nc.vector.tensor_copy(
+                out=wgrp[:, sl].rearrange("p (c i t) -> p c t i", i=4, t=4),
+                in_=wraw[:, sl].rearrange("p (t c i) -> p c t i", t=4, i=4),
+            )
+        nc.vector.quantize_mx(out=wc[:].bitcast(FP8X4), scales=ws[:], in_=wgrp[:])
+
+        transposes(0)
+        quant_hops(0)
+
+        w2grp = consts.tile([P, 2048], BF16, name="w2grp", align_bytes=64)
+        for hh in range(2):
+            xw = psum.tile([P, 1024], BF16, name="xw%d" % hh, tag="xt")
+            for j in range(4):
+                for oo in range(2):
+                    nc.tensor.transpose(
+                        xw[:, j * 256 + oo * P : j * 256 + (oo + 1) * P],
+                        w2raw[:, (2 * hh + oo) * 512 + j * P : (2 * hh + oo) * 512 + (j + 1) * P],
+                        ident_b[:],
+                    )
+            nc.scalar.copy(
+                out=w2grp[:, hh * 1024 : (hh + 1) * 1024].rearrange("p (o j) -> p o j", j=4),
+                in_=xw[:].rearrange("p (j o) -> p o j", j=4),
+            )
+        gbt = psum.tile([P, P], BF16, name="gbt", tag="xt")
+        nc.tensor.transpose(gbt[:], gbraw[:], ident_b[:])
+        gb = consts.tile([P, 8], F32, name="gb")
+        nc.scalar.copy(out=gb[:], in_=gbt[:, 0:8])
+
+        b2bc = consts.tile([P, C], BF16, name="b2bc")
+        b2f = consts.tile([P, C], F32, name="b2f")
+
+        for g in range(NG):
+            if g + 4 < NG:
+                load_group(g + 4)
+            if g + 4 == NG:
+                nc.sync.dma_start(out=b2bc[:], in_=b2.partition_broadcast(P))
+            if g + 1 < NG:
+                transposes(g + 1)
+                quant_hops(g + 1)
+            matmul1(g)
+
+        mv = consts.tile([P, 8], F32, name="mv")
+        for T in range(4):
+            nc.vector.bn_aggr(out=mv[:, 2 * T : 2 * T + 2], in_=stats[:, T * NG * 6 : (T + 1) * NG * 6])
+        mvv = mv[:].rearrange("p (t s) -> p t s", s=2)
+        std = consts.tile([P, 4], F32, name="std")
+        nc.scalar.activation(out=std[:], in_=mvv[:, :, 1], func=ACT.Sqrt, bias=eps[:, 0:1], scale=1.0)
+        rstd = consts.tile([P, 4], F32, name="rstd")
+        nc.vector.reciprocal(out=rstd[:], in_=std[:])
+        sc = consts.tile([P, 4], F32, name="sc")
+        nc.vector.tensor_tensor(out=sc[:], in0=rstd[:], in1=gb[:, 0:4], op=ALU.mult)
+        ms = consts.tile([P, 4], F32, name="ms")
+        nc.vector.tensor_tensor(out=ms[:], in0=mvv[:, :, 0], in1=sc[:], op=ALU.mult)
+        bi = consts.tile([P, 4], F32, name="bi")
+        nc.vector.tensor_tensor(out=bi[:], in0=gb[:, 4:8], in1=ms[:], op=ALU.subtract)
+
+        w2c = consts.tile([P, 512], U32, name="w2c", align_bytes=64)
+        w2s = consts.tile([P, 512], U8, name="w2s", align_bytes=64)
+        nc.vector.quantize_mx(out=w2c[:].bitcast(FP8X4), scales=w2s[:], in_=w2grp[:])
+        nc.vector.tensor_copy(out=b2f[:], in_=b2bc[:])
+
+        order = list(IN_PSUM) + [g for g in range(NG) if g not in IN_PSUM]
+        ycodes = {}
+        yscales = {}
+
+        def norm_quant(g):
+            yp = ypool.tile([P, 2048], BF16, name="yp%d" % g, tag="yp")
+            for T in range(4):
+                nc.scalar.activation(
+                    out=yp[:, T * 512 : (T + 1) * 512],
+                    in_=zsrc[(g, T)],
+                    func=ACT.Relu,
+                    bias=bi[:, T : T + 1],
+                    scale=sc[:, T : T + 1],
+                )
+            ygrp = ypool.tile([P, 2048], BF16, name="ygrp%d" % g, tag="ygrp", align_bytes=64)
+            nc.vector.tensor_copy(
+                out=ygrp[:].rearrange("p (c i t) -> p c t i", i=4, t=4),
+                in_=yp[:].rearrange("p (t c i) -> p c t i", t=4, i=4),
+            )
+            codes = ypool.tile([P, 512], U32, name="yc%d" % g, tag="yc", align_bytes=64)
+            scales = ypool.tile([P, 512], U8, name="ys%d" % g, tag="ys", align_bytes=64)
+            nc.vector.quantize_mx(out=codes[:].bitcast(FP8X4), scales=scales[:], in_=ygrp[:])
+            ycodes[g] = codes
+            yscales[g] = scales
+
+        def matmul2(i, g):
+            osb = opool.tile([P, 2048], F32, name="osb%d" % g, tag="osb")
+            dst = oflat[g * GROUP : (g + 1) * GROUP, :].rearrange("(r t) o -> r (t o)", t=4)
+            for t in range(4):
+                ob = psum.tile([P, 512], F32, name="ob%d_%d" % (g, t), tag=("acc" if i % 2 == 0 else "xt"))
+                nc.tensor.matmul_mx(
+                    out=ob[:],
+                    lhsT=ycodes[g][:, t * P : (t + 1) * P].bitcast(FP8X4),
+                    lhsT_scale=yscales[g][:, t * P : (t + 1) * P],
+                    rhs=w2c[:].bitcast(FP8X4),
+                    rhs_scale=w2s[:],
+                    start=True,
+                    stop=True,
+                )
+                nc.vector.tensor_tensor(out=osb[:, t * 512 : (t + 1) * 512], in0=ob[:], in1=b2f[:], op=ALU.add)
+                if i == NG - 1:
+                    nc.sync.dma_start(out=dst[:, t * 512 : (t + 1) * 512], in_=osb[:, t * 512 : (t + 1) * 512])
+            if i < NG - 1:
+                nc.sync.dma_start(out=dst, in_=osb[:])
+
+        norm_quant(order[0])
+        for i in range(NG):
+            if i + 1 < NG:
+                norm_quant(order[i + 1])
+            matmul2(i, order[i])

@@ -21,6 +21,7 @@ IN_PSUM = (6, 7)
 BN_EPS = 1e-5
 FLOPS = 2 * ROWS * K1 * C + 2 * ROWS * C * C
 MANUAL = True
+V_BLOCKS = 96
 
 
 def tile_ginconvfft_pb_t_kernel(tc, hops, weight, gamma, beta, w2, b2, out):
@@ -35,8 +36,7 @@ def tile_ginconvfft_pb_t_kernel(tc, hops, weight, gamma, beta, w2, b2, out):
         consts = ctx.enter_context(tc.tile_pool(name="consts", bufs=1))
         raws = ctx.enter_context(tc.tile_pool(name="raws", bufs=5))
         grps = ctx.enter_context(tc.tile_pool(name="grps", bufs=3))
-        hq = ctx.enter_context(tc.tile_pool(name="hq", bufs=3))
-        zpool = ctx.enter_context(tc.tile_pool(name="zpool", bufs=1))
+        hq = ctx.enter_context(tc.tile_pool(name="hq", bufs=1))
         ypool = ctx.enter_context(tc.tile_pool(name="ypool", bufs=3))
         opool = ctx.enter_context(tc.tile_pool(name="opool", bufs=3))
         psum = ctx.enter_context(tc.psum_pool(name="psum", bufs=4))
@@ -70,14 +70,14 @@ def tile_ginconvfft_pb_t_kernel(tc, hops, weight, gamma, beta, w2, b2, out):
                 nc.sync.dma_start(out=t[:], in_=src)
             hraw.append(t)
 
-        for g in range(4):
-            load_group(g)
-
+        load_group(0)
         w2raw = consts.tile([P, 2048], BF16, name="w2raw")
-        nc.scalar.dma_start(
+        nc.sync.dma_start(
             out=w2raw[:].rearrange("p (a c) -> p a c", a=4),
             in_=w2.rearrange("(a p) c -> p a c", p=P),
         )
+        for g in range(1, 4):
+            load_group(g)
         nc.scalar.dma_start(out=gbraw[0:4, :], in_=gamma.rearrange("(t p) -> t p", p=P))
         nc.scalar.dma_start(out=gbraw[4:8, :], in_=beta.rearrange("(t p) -> t p", p=P))
         nc.scalar.activation(out=junk[:], in_=eps[:], func=ACT.Sqrt)
@@ -109,8 +109,8 @@ def tile_ginconvfft_pb_t_kernel(tc, hops, weight, gamma, beta, w2, b2, out):
             hgrp[g] = grp
 
         def quant_hops(g):
-            codes = hq.tile([P, 1024], U32, name="hc%d" % g, tag="hc", align_bytes=64)
-            scales = hq.tile([P, 1024], U8, name="hs%d" % g, tag="hs", align_bytes=64)
+            codes = hq.tile([P, 1024], U32, name="hc%d" % g, align_bytes=64)
+            scales = hq.tile([P, 1024], U8, name="hs%d" % g, align_bytes=64)
             nc.vector.quantize_mx(out=codes[:].bitcast(FP8X4), scales=scales[:], in_=hgrp[g][:])
             hcodes[g] = codes
             hscales[g] = scales
@@ -120,14 +120,9 @@ def tile_ginconvfft_pb_t_kernel(tc, hops, weight, gamma, beta, w2, b2, out):
         stats = consts.tile([P, 4 * NG * 6], F32, name="stats")
         zsrc = {}
 
-        def matmul1(g):
-            in_psum = g in IN_PSUM
-            if not in_psum:
-                zt = zpool.tile([P, 2048], F32, name="z%d" % g)
+        def matmul1(g, tag, with_stats):
             for T in range(4):
-                acc = psum.tile(
-                    [P, 512], F32, name="acc%d_%d" % (g, T), tag=("xt" if g == NG - 1 else "acc")
-                )
+                acc = psum.tile([P, 512], F32, name="acc%d_%d" % (g, T), tag=tag)
                 for g2 in range(2):
                     wsl = slice(g2 * 512 + T * P, g2 * 512 + (T + 1) * P)
                     hsl = slice(g2 * 512, (g2 + 1) * 512)
@@ -140,13 +135,10 @@ def tile_ginconvfft_pb_t_kernel(tc, hops, weight, gamma, beta, w2, b2, out):
                         start=(g2 == 0),
                         stop=(g2 == 1),
                     )
-                if in_psum:
-                    zsrc[(g, T)] = acc[:]
-                else:
-                    nc.scalar.copy(out=zt[:, T * 512 : (T + 1) * 512], in_=acc[:])
-                    zsrc[(g, T)] = zt[:, T * 512 : (T + 1) * 512]
-                k = (T * NG + g) * 6
-                nc.vector.bn_stats(out=stats[:, k : k + 6], in_=zsrc[(g, T)])
+                zsrc[(g, T)] = acc
+                if with_stats:
+                    k = (T * NG + g) * 6
+                    nc.vector.bn_stats(out=stats[:, k : k + 6], in_=acc[:])
 
         wgrp = grps.tile([P, 4096], BF16, name="wgrp", tag="grp", align_bytes=64)
         for g2 in range(2):
@@ -155,14 +147,15 @@ def tile_ginconvfft_pb_t_kernel(tc, hops, weight, gamma, beta, w2, b2, out):
                 out=wgrp[:, sl].rearrange("p (c i t) -> p c t i", i=4, t=4),
                 in_=wraw[:, sl].rearrange("p (t c i) -> p c t i", t=4, i=4),
             )
-        nc.vector.quantize_mx(out=wc[:].bitcast(FP8X4), scales=ws[:], in_=wgrp[:])
+            ql = slice(g2 * 512, (g2 + 1) * 512)
+            nc.vector.quantize_mx(out=wc[:, ql].bitcast(FP8X4), scales=ws[:, ql], in_=wgrp[:, sl])
 
         transposes(0)
         quant_hops(0)
 
         w2grp = consts.tile([P, 2048], BF16, name="w2grp", align_bytes=64)
         for hh in range(2):
-            xw = psum.tile([P, 1024], BF16, name="xw%d" % hh, tag="xt")
+            xw = psum.tile([P, 1024], BF16, name="xw%d" % hh, tag="acc")
             for j in range(4):
                 for oo in range(2):
                     nc.tensor.transpose(
@@ -174,7 +167,7 @@ def tile_ginconvfft_pb_t_kernel(tc, hops, weight, gamma, beta, w2, b2, out):
                 out=w2grp[:, hh * 1024 : (hh + 1) * 1024].rearrange("p (o j) -> p o j", j=4),
                 in_=xw[:].rearrange("p (j o) -> p o j", j=4),
             )
-        gbt = psum.tile([P, P], BF16, name="gbt", tag="xt")
+        gbt = psum.tile([P, P], BF16, name="gbt", tag="acc")
         nc.tensor.transpose(gbt[:], gbraw[:], ident_b[:])
         gb = consts.tile([P, 8], F32, name="gb")
         nc.scalar.copy(out=gb[:], in_=gbt[:, 0:8])
@@ -182,15 +175,18 @@ def tile_ginconvfft_pb_t_kernel(tc, hops, weight, gamma, beta, w2, b2, out):
         b2bc = consts.tile([P, C], BF16, name="b2bc")
         b2f = consts.tile([P, C], F32, name="b2f")
 
-        for g in range(NG):
-            if g + 4 < NG:
-                load_group(g + 4)
-            if g + 4 == NG:
-                nc.sync.dma_start(out=b2bc[:], in_=b2.partition_broadcast(P))
+        for g in range(4, NG):
+            load_group(g)
+        nc.sync.dma_start(out=b2bc[:], in_=b2.partition_broadcast(P))
+
+        matmul1(0, "acc", True)
+        transposes(1)
+        quant_hops(1)
+        for g in range(1, NG):
             if g + 1 < NG:
                 transposes(g + 1)
                 quant_hops(g + 1)
-            matmul1(g)
+            matmul1(g, "xt" if g == NG - 1 else "acc", True)
 
         mv = consts.tile([P, 8], F32, name="mv")
         for T in range(4):
@@ -216,32 +212,37 @@ def tile_ginconvfft_pb_t_kernel(tc, hops, weight, gamma, beta, w2, b2, out):
         ycodes = {}
         yscales = {}
 
-        def norm_quant(g):
+        yps = {}
+
+        def norm(g):
             yp = ypool.tile([P, 2048], BF16, name="yp%d" % g, tag="yp")
             for T in range(4):
                 nc.scalar.activation(
                     out=yp[:, T * 512 : (T + 1) * 512],
-                    in_=zsrc[(g, T)],
+                    in_=zsrc[(g, T)][:],
                     func=ACT.Relu,
                     bias=bi[:, T : T + 1],
                     scale=sc[:, T : T + 1],
                 )
+            yps[g] = yp
+
+        def regroup_quant(g):
             ygrp = ypool.tile([P, 2048], BF16, name="ygrp%d" % g, tag="ygrp", align_bytes=64)
-            nc.vector.tensor_copy(
-                out=ygrp[:].rearrange("p (c i t) -> p c t i", i=4, t=4),
-                in_=yp[:].rearrange("p (t c i) -> p c t i", t=4, i=4),
-            )
+            dstv = ygrp[:].rearrange("p (c i t) -> p c t i", i=4, t=4)
+            srcv = yps[g][:].rearrange("p (t c i) -> p c t i", t=4, i=4)
+            nc.scalar.copy(out=dstv[:, V_BLOCKS:128], in_=srcv[:, V_BLOCKS:128])
+            nc.vector.tensor_copy(out=dstv[:, 0:V_BLOCKS], in_=srcv[:, 0:V_BLOCKS])
             codes = ypool.tile([P, 512], U32, name="yc%d" % g, tag="yc", align_bytes=64)
             scales = ypool.tile([P, 512], U8, name="ys%d" % g, tag="ys", align_bytes=64)
             nc.vector.quantize_mx(out=codes[:].bitcast(FP8X4), scales=scales[:], in_=ygrp[:])
             ycodes[g] = codes
             yscales[g] = scales
 
-        def matmul2(i, g):
-            osb = opool.tile([P, 2048], F32, name="osb%d" % g, tag="osb")
-            dst = oflat[g * GROUP : (g + 1) * GROUP, :].rearrange("(r t) o -> r (t o)", t=4)
+        obs = {}
+
+        def matmul2(g):
             for t in range(4):
-                ob = psum.tile([P, 512], F32, name="ob%d_%d" % (g, t), tag=("acc" if i % 2 == 0 else "xt"))
+                ob = psum.tile([P, 512], F32, name="ob%d_%d" % (g, t), tag="acc")
                 nc.tensor.matmul_mx(
                     out=ob[:],
                     lhsT=ycodes[g][:, t * P : (t + 1) * P].bitcast(FP8X4),
@@ -251,14 +252,35 @@ def tile_ginconvfft_pb_t_kernel(tc, hops, weight, gamma, beta, w2, b2, out):
                     start=True,
                     stop=True,
                 )
-                nc.vector.tensor_tensor(out=osb[:, t * 512 : (t + 1) * 512], in0=ob[:], in1=b2f[:], op=ALU.add)
-                if i == NG - 1:
-                    nc.sync.dma_start(out=dst[:, t * 512 : (t + 1) * 512], in_=osb[:, t * 512 : (t + 1) * 512])
-            if i < NG - 1:
+                obs[(g, t)] = ob
+
+        def finish(g, last):
+            osb = opool.tile([P, 2048], F32, name="osb%d" % g, tag="osb")
+            dst = oflat[g * GROUP : (g + 1) * GROUP, :].rearrange("(r t) o -> r (t o)", t=4)
+            for t in range(4):
+                sl = slice(t * 512, (t + 1) * 512)
+                if t < 3 or last:
+                    nc.vector.tensor_tensor(out=osb[:, sl], in0=obs[(g, t)][:], in1=b2f[:], op=ALU.add)
+                else:
+                    nc.scalar.copy(out=osb[:, sl], in_=obs[(g, t)][:])
+                    nc.gpsimd.tensor_tensor(out=osb[:, sl], in0=osb[:, sl], in1=b2f[:], op=ALU.add)
+                if last:
+                    nc.sync.dma_start(out=dst[:, sl], in_=osb[:, sl])
+            if not last:
                 nc.sync.dma_start(out=dst, in_=osb[:])
 
-        norm_quant(order[0])
+        norm(order[0])
+        regroup_quant(order[0])
+        norm(order[1])
+        matmul1(order[2], "xt", False)
+        regroup_quant(order[1])
+        matmul2(order[0])
         for i in range(NG):
+            if i + 2 < NG:
+                norm(order[i + 2])
+                if i + 3 < NG:
+                    matmul1(order[i + 3], "xt", False)
+                regroup_quant(order[i + 2])
             if i + 1 < NG:
-                norm_quant(order[i + 1])
-            matmul2(i, order[i])
+                matmul2(order[i + 1])
+            finish(order[i], i == NG - 1)

@@ -18,10 +18,11 @@ C = 512
 GROUP = 512
 NG = ROWS // GROUP
 IN_PSUM = (6, 7)
+COPIED = (0, 1)
 BN_EPS = 1e-5
 FLOPS = 2 * ROWS * K1 * C + 2 * ROWS * C * C
-MANUAL = True
 V_BLOCKS = 96
+USE_ARS = True
 
 
 def tile_ginconvfft_pb_t_kernel(tc, hops, weight, gamma, beta, w2, b2, out):
@@ -31,12 +32,12 @@ def tile_ginconvfft_pb_t_kernel(tc, hops, weight, gamma, beta, w2, b2, out):
     oflat = out.rearrange("b n o -> (b n) o")
 
     with ExitStack() as ctx:
-        if MANUAL:
-            ctx.enter_context(tc.manual_schedule())
+        ctx.enter_context(tc.manual_schedule())
         consts = ctx.enter_context(tc.tile_pool(name="consts", bufs=1))
         raws = ctx.enter_context(tc.tile_pool(name="raws", bufs=5))
         grps = ctx.enter_context(tc.tile_pool(name="grps", bufs=3))
         hq = ctx.enter_context(tc.tile_pool(name="hq", bufs=1))
+        zpool = ctx.enter_context(tc.tile_pool(name="zpool", bufs=1))
         ypool = ctx.enter_context(tc.tile_pool(name="ypool", bufs=3))
         opool = ctx.enter_context(tc.tile_pool(name="opool", bufs=3))
         psum = ctx.enter_context(tc.psum_pool(name="psum", bufs=4))
@@ -80,7 +81,9 @@ def tile_ginconvfft_pb_t_kernel(tc, hops, weight, gamma, beta, w2, b2, out):
             load_group(g)
         nc.scalar.dma_start(out=gbraw[0:4, :], in_=gamma.rearrange("(t p) -> t p", p=P))
         nc.scalar.dma_start(out=gbraw[4:8, :], in_=beta.rearrange("(t p) -> t p", p=P))
-        nc.scalar.activation(out=junk[:], in_=eps[:], func=ACT.Sqrt)
+        nc.scalar.activation(
+            out=junk[:], in_=eps[:], func=(ACT.Abs_reciprocal_sqrt if USE_ARS else ACT.Sqrt)
+        )
 
         hgrp = {}
         hcodes = {}
@@ -120,8 +123,8 @@ def tile_ginconvfft_pb_t_kernel(tc, hops, weight, gamma, beta, w2, b2, out):
         stats = consts.tile([P, 4 * NG * 6], F32, name="stats")
         zsrc = {}
 
-        def matmul1(g, tag, with_stats):
-            for T in range(4):
+        def matmul1(g, tag, planes):
+            for T in planes:
                 acc = psum.tile([P, 512], F32, name="acc%d_%d" % (g, T), tag=tag)
                 for g2 in range(2):
                     wsl = slice(g2 * 512 + T * P, g2 * 512 + (T + 1) * P)
@@ -135,10 +138,18 @@ def tile_ginconvfft_pb_t_kernel(tc, hops, weight, gamma, beta, w2, b2, out):
                         start=(g2 == 0),
                         stop=(g2 == 1),
                     )
-                zsrc[(g, T)] = acc
-                if with_stats:
-                    k = (T * NG + g) * 6
-                    nc.vector.bn_stats(out=stats[:, k : k + 6], in_=acc[:])
+                zsrc[(g, T)] = acc[:]
+
+        def keep_and_stats(g):
+            banks = [zsrc[(g, T)] for T in range(4)]
+            if g not in IN_PSUM:
+                zt = zpool.tile([P, 512 * len(COPIED)], F32, name="z%d" % g)
+                for n, T in enumerate(COPIED):
+                    nc.scalar.copy(out=zt[:, n * 512 : (n + 1) * 512], in_=banks[T])
+                    zsrc[(g, T)] = zt[:, n * 512 : (n + 1) * 512]
+            for T in range(4):
+                k = (T * NG + g) * 6
+                nc.vector.bn_stats(out=stats[:, k : k + 6], in_=banks[T])
 
         wgrp = grps.tile([P, 4096], BF16, name="wgrp", tag="grp", align_bytes=64)
         for g2 in range(2):
@@ -171,37 +182,58 @@ def tile_ginconvfft_pb_t_kernel(tc, hops, weight, gamma, beta, w2, b2, out):
         nc.tensor.transpose(gbt[:], gbraw[:], ident_b[:])
         gb = consts.tile([P, 8], F32, name="gb")
         nc.scalar.copy(out=gb[:], in_=gbt[:, 0:8])
+        ngam = consts.tile([P, 4], F32, name="ngam")
+        nc.scalar.mul(out=ngam[:], in_=gb[:, 0:4], mul=-1.0)
 
         b2bc = consts.tile([P, C], BF16, name="b2bc")
         b2f = consts.tile([P, C], F32, name="b2f")
-
         for g in range(4, NG):
             load_group(g)
         nc.sync.dma_start(out=b2bc[:], in_=b2.partition_broadcast(P))
 
-        matmul1(0, "acc", True)
+        ALL = (0, 1, 2, 3)
         transposes(1)
         quant_hops(1)
+        matmul1(0, "acc", ALL)
+        keep_and_stats(0)
+        transposes(2)
+        quant_hops(2)
         for g in range(1, NG):
-            if g + 1 < NG:
-                transposes(g + 1)
-                quant_hops(g + 1)
-            matmul1(g, "xt" if g == NG - 1 else "acc", True)
+            if g + 2 < NG:
+                transposes(g + 2)
+            matmul1(g, "xt" if g == NG - 1 else "acc", ALL)
+            keep_and_stats(g)
+            if g + 2 < NG:
+                quant_hops(g + 2)
 
         mv = consts.tile([P, 8], F32, name="mv")
         for T in range(4):
             nc.vector.bn_aggr(out=mv[:, 2 * T : 2 * T + 2], in_=stats[:, T * NG * 6 : (T + 1) * NG * 6])
         mvv = mv[:].rearrange("p (t s) -> p t s", s=2)
-        std = consts.tile([P, 4], F32, name="std")
-        nc.scalar.activation(out=std[:], in_=mvv[:, :, 1], func=ACT.Sqrt, bias=eps[:, 0:1], scale=1.0)
-        rstd = consts.tile([P, 4], F32, name="rstd")
-        nc.vector.reciprocal(out=rstd[:], in_=std[:])
         sc = consts.tile([P, 4], F32, name="sc")
-        nc.vector.tensor_tensor(out=sc[:], in0=rstd[:], in1=gb[:, 0:4], op=ALU.mult)
-        ms = consts.tile([P, 4], F32, name="ms")
-        nc.vector.tensor_tensor(out=ms[:], in0=mvv[:, :, 0], in1=sc[:], op=ALU.mult)
         bi = consts.tile([P, 4], F32, name="bi")
-        nc.vector.tensor_tensor(out=bi[:], in0=gb[:, 4:8], in1=ms[:], op=ALU.subtract)
+        rstd = consts.tile([P, 4], F32, name="rstd")
+        nmg = consts.tile([P, 4], F32, name="nmg")
+        nc.vector.tensor_tensor(out=nmg[:], in0=mvv[:, :, 0], in1=ngam[:], op=ALU.mult)
+        if USE_ARS:
+            nc.scalar.activation(
+                out=rstd[:], in_=mvv[:, :, 1], func=ACT.Abs_reciprocal_sqrt, bias=eps[:, 0:1], scale=1.0
+            )
+        else:
+            std = consts.tile([P, 4], F32, name="std")
+            nc.scalar.activation(out=std[:], in_=mvv[:, :, 1], func=ACT.Sqrt, bias=eps[:, 0:1], scale=1.0)
+            nc.vector.reciprocal(out=rstd[:], in_=std[:])
+        for T in range(4):
+            nc.scalar.activation(
+                out=sc[:, T : T + 1], in_=rstd[:, T : T + 1], func=ACT.Identity, scale=gb[:, T : T + 1]
+            )
+            nc.scalar.activation(
+                out=bi[:, T : T + 1],
+                in_=rstd[:, T : T + 1],
+                func=ACT.Identity,
+                bias=gb[:, 4 + T : 5 + T],
+                scale=nmg[:, T : T + 1],
+            )
 
         w2c = consts.tile([P, 512], U32, name="w2c", align_bytes=64)
         w2s = consts.tile([P, 512], U8, name="w2s", align_bytes=64)
@@ -209,29 +241,42 @@ def tile_ginconvfft_pb_t_kernel(tc, hops, weight, gamma, beta, w2, b2, out):
         nc.vector.tensor_copy(out=b2f[:], in_=b2bc[:])
 
         order = list(IN_PSUM) + [g for g in range(NG) if g not in IN_PSUM]
+        REDONE = tuple([T for T in ALL if T not in COPIED])
         ycodes = {}
         yscales = {}
-
         yps = {}
 
-        def norm(g):
+        def norm(g, on_vector):
             yp = ypool.tile([P, 2048], BF16, name="yp%d" % g, tag="yp")
             for T in range(4):
-                nc.scalar.activation(
-                    out=yp[:, T * 512 : (T + 1) * 512],
-                    in_=zsrc[(g, T)][:],
-                    func=ACT.Relu,
-                    bias=bi[:, T : T + 1],
-                    scale=sc[:, T : T + 1],
-                )
+                if on_vector:
+                    nc.vector.tensor_scalar(
+                        out=yp[:, T * 512 : (T + 1) * 512],
+                        in0=zsrc[(g, T)],
+                        scalar1=sc[:, T : T + 1],
+                        scalar2=bi[:, T : T + 1],
+                        op0=ALU.mult,
+                        op1=ALU.add,
+                    )
+                else:
+                    nc.scalar.activation(
+                        out=yp[:, T * 512 : (T + 1) * 512],
+                        in_=zsrc[(g, T)],
+                        func=ACT.Relu,
+                        bias=bi[:, T : T + 1],
+                        scale=sc[:, T : T + 1],
+                    )
             yps[g] = yp
 
-        def regroup_quant(g):
+        def regroup_quant(g, relu_here):
             ygrp = ypool.tile([P, 2048], BF16, name="ygrp%d" % g, tag="ygrp", align_bytes=64)
             dstv = ygrp[:].rearrange("p (c i t) -> p c t i", i=4, t=4)
             srcv = yps[g][:].rearrange("p (t c i) -> p c t i", t=4, i=4)
-            nc.scalar.copy(out=dstv[:, V_BLOCKS:128], in_=srcv[:, V_BLOCKS:128])
-            nc.vector.tensor_copy(out=dstv[:, 0:V_BLOCKS], in_=srcv[:, 0:V_BLOCKS])
+            if relu_here:
+                nc.vector.tensor_scalar_max(out=dstv, in0=srcv, scalar1=0.0)
+            else:
+                nc.scalar.copy(out=dstv[:, V_BLOCKS:128], in_=srcv[:, V_BLOCKS:128])
+                nc.vector.tensor_copy(out=dstv[:, 0:V_BLOCKS], in_=srcv[:, 0:V_BLOCKS])
             codes = ypool.tile([P, 512], U32, name="yc%d" % g, tag="yc", align_bytes=64)
             scales = ypool.tile([P, 512], U8, name="ys%d" % g, tag="ys", align_bytes=64)
             nc.vector.quantize_mx(out=codes[:].bitcast(FP8X4), scales=scales[:], in_=ygrp[:])
@@ -264,23 +309,21 @@ def tile_ginconvfft_pb_t_kernel(tc, hops, weight, gamma, beta, w2, b2, out):
                 else:
                     nc.scalar.copy(out=osb[:, sl], in_=obs[(g, t)][:])
                     nc.gpsimd.tensor_tensor(out=osb[:, sl], in0=osb[:, sl], in1=b2f[:], op=ALU.add)
-                if last:
-                    nc.sync.dma_start(out=dst[:, sl], in_=osb[:, sl])
-            if not last:
-                nc.sync.dma_start(out=dst, in_=osb[:])
+                nc.sync.dma_start(out=dst[:, sl], in_=osb[:, sl])
 
-        norm(order[0])
-        regroup_quant(order[0])
-        norm(order[1])
-        matmul1(order[2], "xt", False)
-        regroup_quant(order[1])
+        norm(order[0], False)
+        norm(order[1], True)
+        matmul1(order[2], "xt", REDONE)
+        matmul1(order[3], "xt", REDONE)
+        regroup_quant(order[0], False)
+        regroup_quant(order[1], True)
         matmul2(order[0])
-        for i in range(NG):
-            if i + 2 < NG:
-                norm(order[i + 2])
-                if i + 3 < NG:
-                    matmul1(order[i + 3], "xt", False)
-                regroup_quant(order[i + 2])
-            if i + 1 < NG:
-                matmul2(order[i + 1])
-            finish(order[i], i == NG - 1)
+        for j in range(2, NG + 2):
+            if j < NG:
+                norm(order[j], False)
+                if j + 2 < NG:
+                    matmul1(order[j + 2], "xt", REDONE)
+                regroup_quant(order[j], False)
+            if j - 1 < NG:
+                matmul2(order[j - 1])
+            finish(order[j - 2], j - 2 == NG - 1)

@@ -318,12 +318,14 @@ def tile_ginconvfft_pb_t_kernel(tc, hops, weight, gamma, beta, w2, b2, out):
         regroup_quant(order[0], False)
         regroup_quant(order[1], True)
         matmul2(order[0])
-        for j in range(2, NG + 2):
-            if j < NG:
+        order = order + [0, 1, 2, 3, 4, 5, 0, 1]
+        NU = len(order)
+        for j in range(2, NU + 2):
+            if j < NU:
                 norm(order[j], False)
-                if j + 2 < NG:
+                if j + 2 < NU:
                     matmul1(order[j + 2], "xt", REDONE)
                 regroup_quant(order[j], False)
-            if j - 1 < NG:
+            if j - 1 < NU:
                 matmul2(order[j - 1])
-            finish(order[j - 2], j - 2 == NG - 1)
+            finish(order[j - 2], j - 2 == NU - 1)

@@ -21,8 +21,9 @@ IN_PSUM = (6, 7)
 COPIED = (0, 1)
 BN_EPS = 1e-5
 FLOPS = 2 * ROWS * K1 * C + 2 * ROWS * C * C
-V_BLOCKS = 96
+V_BLOCKS = 128
 USE_ARS = True
+S_FROM = 3
 
 
 def tile_ginconvfft_pb_t_kernel(tc, hops, weight, gamma, beta, w2, b2, out):
@@ -275,7 +276,8 @@ def tile_ginconvfft_pb_t_kernel(tc, hops, weight, gamma, beta, w2, b2, out):
             if relu_here:
                 nc.vector.tensor_scalar_max(out=dstv, in0=srcv, scalar1=0.0)
             else:
-                nc.scalar.copy(out=dstv[:, V_BLOCKS:128], in_=srcv[:, V_BLOCKS:128])
+                if V_BLOCKS < 128:
+                    nc.scalar.copy(out=dstv[:, V_BLOCKS:128], in_=srcv[:, V_BLOCKS:128])
                 nc.vector.tensor_copy(out=dstv[:, 0:V_BLOCKS], in_=srcv[:, 0:V_BLOCKS])
             codes = ypool.tile([P, 512], U32, name="yc%d" % g, tag="yc", align_bytes=64)
             scales = ypool.tile([P, 512], U8, name="ys%d" % g, tag="ys", align_bytes=64)
@@ -304,7 +306,7 @@ def tile_ginconvfft_pb_t_kernel(tc, hops, weight, gamma, beta, w2, b2, out):
             dst = oflat[g * GROUP : (g + 1) * GROUP, :].rearrange("(r t) o -> r (t o)", t=4)
             for t in range(4):
                 sl = slice(t * 512, (t + 1) * 512)
-                if t < 3 or last:
+                if t < S_FROM or last:
                     nc.vector.tensor_tensor(out=osb[:, sl], in0=obs[(g, t)][:], in1=b2f[:], op=ALU.add)
                 else:
                     nc.scalar.copy(out=osb[:, sl], in_=obs[(g, t)][:])
@@ -318,14 +320,12 @@ def tile_ginconvfft_pb_t_kernel(tc, hops, weight, gamma, beta, w2, b2, out):
         regroup_quant(order[0], False)
         regroup_quant(order[1], True)
         matmul2(order[0])
-        order = order + [0, 1, 2, 3, 4, 5, 0, 1]
-        NU = len(order)
-        for j in range(2, NU + 2):
-            if j < NU:
+        for j in range(2, NG + 2):
+            if j < NG:
                 norm(order[j], False)
-                if j + 2 < NU:
+                if j + 2 < NG:
                     matmul1(order[j + 2], "xt", REDONE)
                 regroup_quant(order[j], False)
-            if j - 1 < NU:
+            if j - 1 < NG:
                 matmul2(order[j - 1])
-            finish(order[j - 2], j - 2 == NU - 1)
+            finish(order[j - 2], j - 2 == NG - 1)

@@ -21,7 +21,7 @@ IN_PSUM = (6, 7)
 COPIED = (0, 1)
 BN_EPS = 1e-5
 FLOPS = 2 * ROWS * K1 * C + 2 * ROWS * C * C
-V_BLOCKS = 128
+V_BLOCKS = 96
 USE_ARS = True
 S_FROM = 3
 
@@ -269,7 +269,9 @@ def tile_ginconvfft_pb_t_kernel(tc, hops, weight, gamma, beta, w2, b2, out):
                     )
             yps[g] = yp
 
-        def regroup_quant(g, relu_here):
+        ygrps = {}
+
+        def regroup(g, relu_here):
             ygrp = ypool.tile([P, 2048], BF16, name="ygrp%d" % g, tag="ygrp", align_bytes=64)
             dstv = ygrp[:].rearrange("p (c i t) -> p c t i", i=4, t=4)
             srcv = yps[g][:].rearrange("p (t c i) -> p c t i", t=4, i=4)
@@ -279,6 +281,10 @@ def tile_ginconvfft_pb_t_kernel(tc, hops, weight, gamma, beta, w2, b2, out):
                 if V_BLOCKS < 128:
                     nc.scalar.copy(out=dstv[:, V_BLOCKS:128], in_=srcv[:, V_BLOCKS:128])
                 nc.vector.tensor_copy(out=dstv[:, 0:V_BLOCKS], in_=srcv[:, 0:V_BLOCKS])
+            ygrps[g] = ygrp
+
+        def quant_y(g):
+            ygrp = ygrps[g]
             codes = ypool.tile([P, 512], U32, name="yc%d" % g, tag="yc", align_bytes=64)
             scales = ypool.tile([P, 512], U8, name="ys%d" % g, tag="ys", align_bytes=64)
             nc.vector.quantize_mx(out=codes[:].bitcast(FP8X4), scales=scales[:], in_=ygrp[:])
@@ -301,10 +307,14 @@ def tile_ginconvfft_pb_t_kernel(tc, hops, weight, gamma, beta, w2, b2, out):
                 )
                 obs[(g, t)] = ob
 
-        def finish(g, last):
-            osb = opool.tile([P, 2048], F32, name="osb%d" % g, tag="osb")
+        osbs = {}
+
+        def finish(g, last, tiles):
+            if g not in osbs:
+                osbs[g] = opool.tile([P, 2048], F32, name="osb%d" % g, tag="osb")
+            osb = osbs[g]
             dst = oflat[g * GROUP : (g + 1) * GROUP, :].rearrange("(r t) o -> r (t o)", t=4)
-            for t in range(4):
+            for t in tiles:
                 sl = slice(t * 512, (t + 1) * 512)
                 if t < S_FROM or last:
                     nc.vector.tensor_tensor(out=osb[:, sl], in0=obs[(g, t)][:], in1=b2f[:], op=ALU.add)
@@ -317,15 +327,22 @@ def tile_ginconvfft_pb_t_kernel(tc, hops, weight, gamma, beta, w2, b2, out):
         norm(order[1], True)
         matmul1(order[2], "xt", REDONE)
         matmul1(order[3], "xt", REDONE)
-        regroup_quant(order[0], False)
-        regroup_quant(order[1], True)
+        regroup(order[0], False)
+        regroup(order[1], True)
+        quant_y(order[0])
+        quant_y(order[1])
         matmul2(order[0])
         for j in range(2, NG + 2):
+            last = j - 2 == NG - 1
             if j < NG:
                 norm(order[j], False)
                 if j + 2 < NG:
                     matmul1(order[j + 2], "xt", REDONE)
-                regroup_quant(order[j], False)
+                regroup(order[j], False)
+                finish(order[j - 2], last, (0,))
+                quant_y(order[j])
+            else:
+                finish(order[j - 2], last, (0,))
             if j - 1 < NG:
                 matmul2(order[j - 1])
-            finish(order[j - 2], j - 2 == NG - 1)
+            finish(order[j - 2], last, (1, 2, 3))

@@ -33,7 +33,6 @@ def tile_ginconvfft_pb_t_kernel(tc, hops, weight, gamma, beta, w2, b2, out):
     oflat = out.rearrange("b n o -> (b n) o")
 
     with ExitStack() as ctx:
-        ctx.enter_context(tc.manual_schedule())
         consts = ctx.enter_context(tc.tile_pool(name="consts", bufs=1))
         raws = ctx.enter_context(tc.tile_pool(name="raws", bufs=5))
         grps = ctx.enter_context(tc.tile_pool(name="grps", bufs=3))

@@ -155,8 +155,8 @@ def tile_ginconvfft_pb_t_kernel(tc, hops, weight, gamma, beta, w2, b2, out):
         for g2 in range(2):
             sl = slice(g2 * 2048, (g2 + 1) * 2048)
             nc.vector.tensor_copy(
-                out=wgrp[:, sl].rearrange("p (c i t) -> p c t i", i=4, t=4),
-                in_=wraw[:, sl].rearrange("p (t c i) -> p c t i", t=4, i=4),
+                out=wgrp[:, sl].rearrange("p (c t) -> p c t", t=4),
+                in_=wraw[:, sl].rearrange("p (t c) -> p c t", t=4),
             )
             ql = slice(g2 * 512, (g2 + 1) * 512)
             nc.vector.quantize_mx(out=wc[:, ql].bitcast(FP8X4), scales=ws[:, ql], in_=wgrp[:, sl])
@@ -274,12 +274,14 @@ def tile_ginconvfft_pb_t_kernel(tc, hops, weight, gamma, beta, w2, b2, out):
             ygrp = ypool.tile([P, 2048], BF16, name="ygrp%d" % g, tag="ygrp", align_bytes=64)
             dstv = ygrp[:].rearrange("p (c i t) -> p c t i", i=4, t=4)
             srcv = yps[g][:].rearrange("p (t c i) -> p c t i", t=4, i=4)
+            dstw = ygrp[:].rearrange("p (c t) -> p c t", t=4)
+            srcw = yps[g][:].rearrange("p (t c) -> p c t", t=4)
             if relu_here:
-                nc.vector.tensor_scalar_max(out=dstv, in0=srcv, scalar1=0.0)
+                nc.vector.tensor_scalar_max(out=dstw, in0=srcw, scalar1=0.0)
             else:
                 if V_BLOCKS < 128:
                     nc.scalar.copy(out=dstv[:, V_BLOCKS:128], in_=srcv[:, V_BLOCKS:128])
-                nc.vector.tensor_copy(out=dstv[:, 0:V_BLOCKS], in_=srcv[:, 0:V_BLOCKS])
+                nc.vector.tensor_copy(out=dstw[:, 0 : 4 * V_BLOCKS, :], in_=srcw[:, 0 : 4 * V_BLOCKS, :])
             ygrps[g] = ygrp
 
         def quant_y(g):

from contextlib import ExitStack

import concourse.mybir as mybir
from concourse.masks import make_identity

F32 = mybir.dt.float32
BF16 = mybir.dt.bfloat16
U32 = mybir.dt.uint32
U8 = mybir.dt.uint8
FP8X4 = mybir.dt.float8_e4m3fn_x4
ACT = mybir.ActivationFunctionType
ALU = mybir.AluOpType

P = 128
ROWS = 4096
K1 = 1024
C = 512
GROUP = 512
NG = ROWS // GROUP
IN_PSUM = (6, 7)
COPIED = (0, 1)
BN_EPS = 1e-5
FLOPS = 2 * ROWS * K1 * C + 2 * ROWS * C * C
V_BLOCKS = 96
USE_ARS = True
S_FROM = 3


def tile_ginconvfft_pb_t_kernel(tc, hops, weight, gamma, beta, w2, b2, out):
    nc = tc.nc
    hflat = hops.rearrange("b n l m -> (b n) (l m)")
    wflat = weight.rearrange("l m c -> (l m) c")
    oflat = out.rearrange("b n o -> (b n) o")

    with ExitStack() as ctx:
        consts = ctx.enter_context(tc.tile_pool(name="consts", bufs=1))
        raws = ctx.enter_context(tc.tile_pool(name="raws", bufs=5))
        grps = ctx.enter_context(tc.tile_pool(name="grps", bufs=3))
        hq = ctx.enter_context(tc.tile_pool(name="hq", bufs=1))
        zpool = ctx.enter_context(tc.tile_pool(name="zpool", bufs=1))
        ypool = ctx.enter_context(tc.tile_pool(name="ypool", bufs=3))
        opool = ctx.enter_context(tc.tile_pool(name="opool", bufs=3))
        psum = ctx.enter_context(tc.psum_pool(name="psum", bufs=4))

        eps = consts.tile([P, 1], F32, name="eps")
        nc.vector.memset(eps[:], BN_EPS)
        junk = consts.tile([P, 1], F32, name="junk")
        ident_f = consts.tile([P, P], F32, name="ident_f")
        make_identity(nc, ident_f[:])
        ident_b = consts.tile([P, P], BF16, name="ident_b")
        make_identity(nc, ident_b[:])
        gbraw = consts.tile([P, P], BF16, name="gbraw")
        nc.gpsimd.memset(gbraw[:], 0.0)

        wraw = raws.tile([P, 4096], BF16, name="wraw", tag="raw")
        wview = wflat.rearrange("(a p e) c -> p a (e c)", a=4, p=P, e=2)
        for g2 in range(2):
            nc.sync.dma_start(
                out=wraw[:, g2 * 2048 : (g2 + 1) * 2048].rearrange("p (a x) -> p a x", a=2),
                in_=wview[:, 2 * g2 : 2 * g2 + 2, :],
            )
        hraw = []

        def load_group(g):
            t = raws.tile([P, 4096], BF16, name="hraw%d" % g, tag="raw")
            src = hflat[g * GROUP : (g + 1) * GROUP, :].rearrange("(p t) k -> p (t k)", t=4)
            if g == 0:
                nc.sync.dma_start(out=t[:, 0:2048], in_=src[:, 0:2048])
                nc.sync.dma_start(out=t[:, 2048:4096], in_=src[:, 2048:4096])
            else:
                nc.sync.dma_start(out=t[:], in_=src)
            hraw.append(t)

        load_group(0)
        w2raw = consts.tile([P, 2048], BF16, name="w2raw")
        nc.sync.dma_start(
            out=w2raw[:].rearrange("p (a c) -> p a c", a=4),
            in_=w2.rearrange("(a p) c -> p a c", p=P),
        )
        for g in range(1, 4):
            load_group(g)
        nc.scalar.dma_start(out=gbraw[0:4, :], in_=gamma.rearrange("(t p) -> t p", p=P))
        nc.scalar.dma_start(out=gbraw[4:8, :], in_=beta.rearrange("(t p) -> t p", p=P))
        nc.scalar.activation(
            out=junk[:], in_=eps[:], func=(ACT.Abs_reciprocal_sqrt if USE_ARS else ACT.Sqrt)
        )

        hgrp = {}
        hcodes = {}
        hscales = {}

        def transposes(g):
            rawf = hraw[g][:].bitcast(F32)
            grp = grps.tile([P, 4096], BF16, name="hgrp%d" % g, tag="grp", align_bytes=64)
            grpf = grp[:].bitcast(F32)
            for h in range(2):
                for g2 in range(2):
                    xt = psum.tile([P, 512], F32, name="xt%d_%d%d" % (g, h, g2), tag="xt")
                    for u in range(2):
                        for tt in range(2):
                            col = (2 * h + tt) * 512 + (2 * g2 + u) * P
                            nc.tensor.transpose(
                                xt[:, (2 * u + tt) * P : (2 * u + tt + 1) * P],
                                rawf[:, col : col + P],
                                ident_f[:],
                            )
                    lo = g2 * 1024 + h * 512
                    nc.scalar.copy(
                        out=grpf[:, lo : lo + 512].rearrange("p (x u) -> p x u", u=2),
                        in_=xt[:].rearrange("p (u x) -> p x u", u=2),
                    )
            hgrp[g] = grp

        def quant_hops(g):
            codes = hq.tile([P, 1024], U32, name="hc%d" % g, align_bytes=64)
            scales = hq.tile([P, 1024], U8, name="hs%d" % g, align_bytes=64)
            nc.vector.quantize_mx(out=codes[:].bitcast(FP8X4), scales=scales[:], in_=hgrp[g][:])
            hcodes[g] = codes
            hscales[g] = scales

        wc = consts.tile([P, 1024], U32, name="wc", align_bytes=64)
        ws = consts.tile([P, 1024], U8, name="ws", align_bytes=64)
        stats = consts.tile([P, 4 * NG * 6], F32, name="stats")
        zsrc = {}

        def matmul1(g, tag, planes):
            for T in planes:
                acc = psum.tile([P, 512], F32, name="acc%d_%d" % (g, T), tag=tag)
                for g2 in range(2):
                    wsl = slice(g2 * 512 + T * P, g2 * 512 + (T + 1) * P)
                    hsl = slice(g2 * 512, (g2 + 1) * 512)
                    nc.tensor.matmul_mx(
                        out=acc[:],
                        lhsT=wc[:, wsl].bitcast(FP8X4),
                        lhsT_scale=ws[:, wsl],
                        rhs=hcodes[g][:, hsl].bitcast(FP8X4),
                        rhs_scale=hscales[g][:, hsl],
                        start=(g2 == 0),
                        stop=(g2 == 1),
                    )
                zsrc[(g, T)] = acc[:]

        def keep_and_stats(g):
            banks = [zsrc[(g, T)] for T in range(4)]
            if g not in IN_PSUM:
                zt = zpool.tile([P, 512 * len(COPIED)], F32, name="z%d" % g)
                for n, T in enumerate(COPIED):
                    nc.scalar.copy(out=zt[:, n * 512 : (n + 1) * 512], in_=banks[T])
                    zsrc[(g, T)] = zt[:, n * 512 : (n + 1) * 512]
            for T in range(4):
                k = (T * NG + g) * 6
                nc.vector.bn_stats(out=stats[:, k : k + 6], in_=banks[T])

        wgrp = grps.tile([P, 4096], BF16, name="wgrp", tag="grp", align_bytes=64)
        for g2 in range(2):
            sl = slice(g2 * 2048, (g2 + 1) * 2048)
            nc.vector.tensor_copy(
                out=wgrp[:, sl].rearrange("p (c t) -> p c t", t=4),
                in_=wraw[:, sl].rearrange("p (t c) -> p c t", t=4),
            )
            ql = slice(g2 * 512, (g2 + 1) * 512)
            nc.vector.quantize_mx(out=wc[:, ql].bitcast(FP8X4), scales=ws[:, ql], in_=wgrp[:, sl])

        transposes(0)
        quant_hops(0)

        w2grp = consts.tile([P, 2048], BF16, name="w2grp", align_bytes=64)
        for hh in range(2):
            xw = psum.tile([P, 1024], BF16, name="xw%d" % hh, tag="acc")
            for j in range(4):
                for oo in range(2):
                    nc.tensor.transpose(
                        xw[:, j * 256 + oo * P : j * 256 + (oo + 1) * P],
                        w2raw[:, (2 * hh + oo) * 512 + j * P : (2 * hh + oo) * 512 + (j + 1) * P],
                        ident_b[:],
                    )
            nc.scalar.copy(
                out=w2grp[:, hh * 1024 : (hh + 1) * 1024].rearrange("p (o j) -> p o j", j=4),
                in_=xw[:].rearrange("p (j o) -> p o j", j=4),
            )
        gbt = psum.tile([P, P], BF16, name="gbt", tag="acc")
        nc.tensor.transpose(gbt[:], gbraw[:], ident_b[:])
        gb = consts.tile([P, 8], F32, name="gb")
        nc.scalar.copy(out=gb[:], in_=gbt[:, 0:8])
        ngam = consts.tile([P, 4], F32, name="ngam")
        nc.scalar.mul(out=ngam[:], in_=gb[:, 0:4], mul=-1.0)

        b2bc = consts.tile([P, C], BF16, name="b2bc")
        b2f = consts.tile([P, C], F32, name="b2f")
        for g in range(4, NG):
            load_group(g)
        nc.sync.dma_start(out=b2bc[:], in_=b2.partition_broadcast(P))

        ALL = (0, 1, 2, 3)
        transposes(1)
        quant_hops(1)
        matmul1(0, "acc", ALL)
        keep_and_stats(0)
        transposes(2)
        quant_hops(2)
        for g in range(1, NG):
            if g + 2 < NG:
                transposes(g + 2)
            matmul1(g, "xt" if g == NG - 1 else "acc", ALL)
            keep_and_stats(g)
            if g + 2 < NG:
                quant_hops(g + 2)

        mv = consts.tile([P, 8], F32, name="mv")
        for T in range(4):
            nc.vector.bn_aggr(out=mv[:, 2 * T : 2 * T + 2], in_=stats[:, T * NG * 6 : (T + 1) * NG * 6])
        mvv = mv[:].rearrange("p (t s) -> p t s", s=2)
        sc = consts.tile([P, 4], F32, name="sc")
        bi = consts.tile([P, 4], F32, name="bi")
        rstd = consts.tile([P, 4], F32, name="rstd")
        nmg = consts.tile([P, 4], F32, name="nmg")
        nc.vector.tensor_tensor(out=nmg[:], in0=mvv[:, :, 0], in1=ngam[:], op=ALU.mult)
        if USE_ARS:
            nc.scalar.activation(
                out=rstd[:], in_=mvv[:, :, 1], func=ACT.Abs_reciprocal_sqrt, bias=eps[:, 0:1], scale=1.0
            )
        else:
            std = consts.tile([P, 4], F32, name="std")
            nc.scalar.activation(out=std[:], in_=mvv[:, :, 1], func=ACT.Sqrt, bias=eps[:, 0:1], scale=1.0)
            nc.vector.reciprocal(out=rstd[:], in_=std[:])
        for T in range(4):
            nc.scalar.activation(
                out=sc[:, T : T + 1], in_=rstd[:, T : T + 1], func=ACT.Identity, scale=gb[:, T : T + 1]
            )
            nc.scalar.activation(
                out=bi[:, T : T + 1],
                in_=rstd[:, T : T + 1],
                func=ACT.Identity,
                bias=gb[:, 4 + T : 5 + T],
                scale=nmg[:, T : T + 1],
            )

        w2c = consts.tile([P, 512], U32, name="w2c", align_bytes=64)
        w2s = consts.tile([P, 512], U8, name="w2s", align_bytes=64)
        nc.vector.quantize_mx(out=w2c[:].bitcast(FP8X4), scales=w2s[:], in_=w2grp[:])
        nc.vector.tensor_copy(out=b2f[:], in_=b2bc[:])

        order = list(IN_PSUM) + [g for g in range(NG) if g not in IN_PSUM]
        REDONE = tuple([T for T in ALL if T not in COPIED])
        ycodes = {}
        yscales = {}
        yps = {}

        def norm(g, on_vector):
            yp = ypool.tile([P, 2048], BF16, name="yp%d" % g, tag="yp")
            for T in range(4):
                if on_vector:
                    nc.vector.tensor_scalar(
                        out=yp[:, T * 512 : (T + 1) * 512],
                        in0=zsrc[(g, T)],
                        scalar1=sc[:, T : T + 1],
                        scalar2=bi[:, T : T + 1],
                        op0=ALU.mult,
                        op1=ALU.add,
                    )
                else:
                    nc.scalar.activation(
                        out=yp[:, T * 512 : (T + 1) * 512],
                        in_=zsrc[(g, T)],
                        func=ACT.Relu,
                        bias=bi[:, T : T + 1],
                        scale=sc[:, T : T + 1],
                    )
            yps[g] = yp

        ygrps = {}

        def regroup(g, relu_here):
            ygrp = ypool.tile([P, 2048], BF16, name="ygrp%d" % g, tag="ygrp", align_bytes=64)
            dstv = ygrp[:].rearrange("p (c i t) -> p c t i", i=4, t=4)
            srcv = yps[g][:].rearrange("p (t c i) -> p c t i", t=4, i=4)
            dstw = ygrp[:].rearrange("p (c t) -> p c t", t=4)
            srcw = yps[g][:].rearrange("p (t c) -> p c t", t=4)
            if relu_here:
                nc.vector.tensor_scalar_max(out=dstw, in0=srcw, scalar1=0.0)
            else:
                if V_BLOCKS < 128:
                    nc.scalar.copy(out=dstv[:, V_BLOCKS:128], in_=srcv[:, V_BLOCKS:128])
                nc.vector.tensor_copy(out=dstw[:, 0 : 4 * V_BLOCKS, :], in_=srcw[:, 0 : 4 * V_BLOCKS, :])
            ygrps[g] = ygrp

        def quant_y(g):
            ygrp = ygrps[g]
            codes = ypool.tile([P, 512], U32, name="yc%d" % g, tag="yc", align_bytes=64)
            scales = ypool.tile([P, 512], U8, name="ys%d" % g, tag="ys", align_bytes=64)
            nc.vector.quantize_mx(out=codes[:].bitcast(FP8X4), scales=scales[:], in_=ygrp[:])
            ycodes[g] = codes
            yscales[g] = scales

        obs = {}

        def matmul2(g):
            for t in range(4):
                ob = psum.tile([P, 512], F32, name="ob%d_%d" % (g, t), tag="acc")
                nc.tensor.matmul_mx(
                    out=ob[:],
                    lhsT=ycodes[g][:, t * P : (t + 1) * P].bitcast(FP8X4),
                    lhsT_scale=yscales[g][:, t * P : (t + 1) * P],
                    rhs=w2c[:].bitcast(FP8X4),
                    rhs_scale=w2s[:],
                    start=True,
                    stop=True,
                )
                obs[(g, t)] = ob

        osbs = {}

        def finish(g, last, tiles):
            if g not in osbs:
                osbs[g] = opool.tile([P, 2048], F32, name="osb%d" % g, tag="osb")
            osb = osbs[g]
            dst = oflat[g * GROUP : (g + 1) * GROUP, :].rearrange("(r t) o -> r (t o)", t=4)
            for t in tiles:
                sl = slice(t * 512, (t + 1) * 512)
                if t < S_FROM or last:
                    nc.vector.tensor_tensor(out=osb[:, sl], in0=obs[(g, t)][:], in1=b2f[:], op=ALU.add)
                else:
                    nc.scalar.copy(out=osb[:, sl], in_=obs[(g, t)][:])
                    nc.gpsimd.tensor_tensor(out=osb[:, sl], in0=osb[:, sl], in1=b2f[:], op=ALU.add)
                nc.sync.dma_start(out=dst[:, sl], in_=osb[:, sl])

        norm(order[0], False)
        norm(order[1], True)
        matmul1(order[2], "xt", REDONE)
        matmul1(order[3], "xt", REDONE)
        regroup(order[0], False)
        regroup(order[1], True)
        quant_y(order[0])
        quant_y(order[1])
        matmul2(order[0])
        for j in range(2, NG + 2):
            last = j - 2 == NG - 1
            if j < NG:
                norm(order[j], False)
                if j + 2 < NG:
                    matmul1(order[j + 2], "xt", REDONE)
                regroup(order[j], False)
                finish(order[j - 2], last, (0,))
                quant_y(order[j])
            else:
                finish(order[j - 2], last, (0,))
            if j - 1 < NG:
                matmul2(order[j - 1])
            finish(order[j - 2], last, (1, 2, 3))
